import numpy as np
import ml_dtypes


def mxq(x, axis, fmt="e4m3"):
    dtype, down = {"e4m3": (ml_dtypes.float8_e4m3fn, 7), "e5m2": (ml_dtypes.float8_e5m2, 14)}[fmt]
    v = np.moveaxis(np.asarray(x, np.float32).astype(ml_dtypes.bfloat16).astype(np.float64), axis, -1)
    blocks = v.reshape(v.shape[:-1] + (-1, 32))
    amax = np.abs(blocks).max(-1, keepdims=True)
    byte = np.maximum(np.where(amax > 0, np.frexp(amax)[1] - 1 + 127, 0) - down, 1)
    scale = np.exp2(byte - 127.0)
    codes = (blocks / scale).astype(np.float32).astype(dtype).astype(np.float64)
    return np.moveaxis((codes * scale).reshape(v.shape), -1, axis)


WIDE = False


def mx_kscale(k):
    if not WIDE:
        return np.ones(k)
    levels = np.array([10, -10, 5, -5, 0])
    a = np.random.permutation(np.resize(levels, k // 512 * 4)).reshape(k // 512, 4)
    idx = np.arange(k)
    return np.exp2(a[idx // 512, idx % 128 // 32])


BF16 = ml_dtypes.bfloat16


def bf(x):
    return np.asarray(x, np.float32).astype(BF16)


def f64(x):
    return np.asarray(x).astype(np.float64)


B, L, S, D, DA, H, MLP = 4, 3, 2048, 256, 512, 16, 4096
EPS = 1e-5


def layer_norm(u, g, b):
    mu = u.mean(-1, keepdims=True)
    var = ((u - mu) ** 2).mean(-1, keepdims=True)
    return (u - mu) / np.sqrt(var + EPS) * g + b


def setup_inputs():
    s = mx_kscale(DA)
    r = np.random.standard_normal
    return {"h_attn": bf(r((B, S, DA)) * 2.0 * s), "x": bf(r((B, S, D))),
            "attn_out_W": bf(r((DA, D)) * 0.5 / np.sqrt(DA) / s[:, None]), "attn_out_b": bf(r(D) * 0.2),
            "attn_norm_g": bf(1.0 + 0.1 * r(D)), "attn_norm_b": bf(r(D) * 0.1)}


def reference(h_attn, x, attn_out_W, attn_out_b, attn_norm_g, attn_norm_b):
    o = (mxq(f64(h_attn), 2, "e4m3") @ mxq(f64(attn_out_W), 0, "e4m3")) + f64(attn_out_b)
    return f64(x) + layer_norm(o, f64(attn_norm_g), f64(attn_norm_b))

@@ -1,0 +1,223 @@
+from contextlib import ExitStack
+
+import concourse.mybir as mybir
+from concourse.masks import make_identity
+
+F32 = mybir.dt.float32
+BF16 = mybir.dt.bfloat16
+U32 = mybir.dt.uint32
+U8 = mybir.dt.uint8
+FP8X4 = mybir.dt.float8_e4m3fn_x4
+ALU = mybir.AluOpType
+ACT = mybir.ActivationFunctionType
+
+P = 128
+PACK = 4
+ROWS = 4 * 2048
+K = 512
+FEAT = 256
+HALVES = FEAT // P
+WORDS = K // 2
+TILES = ROWS // P
+GROUP = 4
+PAIR = 2
+GROUPS = TILES // GROUP
+EPS = 1e-5
+
+FLOPS = 2 * ROWS * K * FEAT
+
+
+def tile_dcadecoderblock_pb_t_kernel(
+    tc, h_attn, x, attn_out_W, attn_out_b, attn_norm_g, attn_norm_b, out
+):
+    nc = tc.nc
+    h_rows = h_attn.flatten_outer_dims().rearrange("(p j) k -> p j k", j=TILES)
+    x_rows = x.flatten_outer_dims().rearrange("(p j) n -> p j n", j=TILES)
+    out_rows = out.flatten_outer_dims().rearrange("(p j) n -> p j n", j=TILES)
+
+    with ExitStack() as stack:
+        consts = stack.enter_context(tc.tile_pool(name="consts", bufs=1))
+        loads = stack.enter_context(tc.tile_pool(name="loads", bufs=GROUPS))
+        work = stack.enter_context(tc.tile_pool(name="work", bufs=3))
+        stats = stack.enter_context(tc.tile_pool(name="stats", bufs=4))
+        psum = stack.enter_context(tc.psum_pool(name="psum", bufs=2))
+
+        h_tiles = []
+        x_tiles = []
+        for g in range(GROUPS):
+            tiles = slice(g * GROUP, (g + 1) * GROUP)
+            h_sb = loads.tile([P, GROUP * K], BF16)
+            nc.sync.dma_start(
+                out=h_sb[:].rearrange("p (i k) -> p i k", i=GROUP), in_=h_rows[:, tiles, :]
+            )
+            h_tiles.append(h_sb)
+            x_sb = loads.tile([P, GROUP * FEAT], BF16)
+            nc.sync.dma_start(
+                out=x_sb[:].rearrange("p (i n) -> p i n", i=GROUP), in_=x_rows[:, tiles, :]
+            )
+            x_tiles.append(x_sb)
+
+        eps = consts.tile([P, 1], F32)
+        nc.vector.memset(eps[:], EPS)
+        table_warm = consts.tile([P, 1], F32)
+        nc.scalar.activation(out=table_warm[:], in_=eps[:], func=ACT.Sqrt)
+
+        ident = consts.tile([P, P], F32)
+        make_identity(nc, ident[:])
+
+        w_raw = consts.tile([P, PACK, FEAT], BF16)
+        nc.scalar.dma_start(
+            out=w_raw[:].rearrange("p (u e) n -> p u e n", u=2),
+            in_=attn_out_W.rearrange("(u p e) n -> p u e n", u=2, e=2),
+        )
+        w_grouped = consts.tile([P, FEAT, PACK], BF16, align_bytes=64)
+        nc.vector.tensor_copy(out=w_grouped[:], in_=w_raw[:].rearrange("p t n -> p n t"))
+        w_codes = consts.tile([P, FEAT], U32, align_bytes=64)
+        w_scales = consts.tile([P, FEAT], U8, align_bytes=64)
+        nc.vector.quantize_mx(
+            out=w_codes[:].bitcast(FP8X4),
+            scales=w_scales[:],
+            in_=w_grouped[:].rearrange("p n t -> p (n t)"),
+        )
+
+        ones = consts.tile([P, P], BF16)
+        nc.vector.memset(ones[:], 1.0)
+        bias_row = consts.tile([P, FEAT], BF16)
+        nc.vector.memset(bias_row[:], 0.0)
+        nc.scalar.dma_start(out=bias_row[0:1, :], in_=attn_out_b.rearrange("(o n) -> o n", o=1))
+        bias_ps = psum.tile([P, FEAT], F32, tag="a_ps")
+        nc.tensor.matmul(out=bias_ps[:], lhsT=ones[:], rhs=bias_row[:], start=True, stop=True)
+        bias_all = consts.tile([P, FEAT], F32)
+        nc.vector.tensor_copy(out=bias_all[:], in_=bias_ps[:])
+
+        norm_rows = consts.tile([P, P], BF16)
+        nc.vector.memset(norm_rows[:], 0.0)
+        nc.scalar.dma_start(
+            out=norm_rows[0:HALVES, :], in_=attn_norm_g.rearrange("(j p) -> j p", p=P)
+        )
+        nc.scalar.dma_start(
+            out=norm_rows[HALVES : 2 * HALVES, :], in_=attn_norm_b.rearrange("(j p) -> j p", p=P)
+        )
+        norm_rows_f32 = consts.tile([P, P], F32)
+        nc.vector.tensor_copy(out=norm_rows_f32[:], in_=norm_rows[:])
+        norm_ps = psum.tile([P, P], F32, tag="tT_ps")
+        nc.tensor.transpose(norm_ps[:], norm_rows_f32[:], ident[:])
+        norm_cols = consts.tile([P, 2 * HALVES], F32)
+        nc.vector.tensor_copy(out=norm_cols[:], in_=norm_ps[:, 0 : 2 * HALVES])
+
+        for g in range(GROUPS):
+            h_words = h_tiles[g][:].bitcast(F32)
+            grouped = work.tile([P, GROUP * P * PACK], BF16, align_bytes=64)
+            grouped_words = grouped[:].bitcast(F32)
+            for pair in range(GROUP // PAIR):
+                hT_ps = psum.tile([P, PAIR * WORDS], F32)
+                for c in range(PAIR * WORDS // P):
+                    src = pair * PAIR * WORDS + c * P
+                    nc.tensor.transpose(
+                        hT_ps[:, c * P : (c + 1) * P], h_words[:, src : src + P], ident[:]
+                    )
+                nc.scalar.copy(
+                    out=grouped_words[:, pair * PAIR * WORDS : (pair + 1) * PAIR * WORDS].rearrange(
+                        "p (i r u) -> p i r u", i=PAIR, u=2
+                    ),
+                    in_=hT_ps[:].rearrange("p (i u r) -> p i r u", i=PAIR, u=2),
+                )
+
+            h_codes = work.tile([P, GROUP * P], U32, align_bytes=64)
+            h_scales = work.tile([P, GROUP * P], U8, align_bytes=64)
+            nc.vector.quantize_mx(
+                out=h_codes[:].bitcast(FP8X4), scales=h_scales[:], in_=grouped[:]
+            )
+
+            o = work.tile([P, GROUP, FEAT], F32)
+            row_sum = stats.tile([P, GROUP], F32)
+            for pair in range(GROUP // PAIR):
+                a_ps = psum.tile([P, PAIR, FEAT], F32)
+                for i2 in range(PAIR):
+                    rows = slice((pair * PAIR + i2) * P, (pair * PAIR + i2 + 1) * P)
+                    nc.tensor.matmul_mx(
+                        out=a_ps[:, i2, :],
+                        lhsT=h_codes[:, rows].bitcast(FP8X4),
+                        lhsT_scale=h_scales[:, rows],
+                        rhs=w_codes[:].bitcast(FP8X4),
+                        rhs_scale=w_scales[:],
+                        start=True,
+                        stop=True,
+                    )
+                for i2 in range(PAIR):
+                    i = pair * PAIR + i2
+                    nc.vector.scalar_tensor_tensor(
+                        out=o[:, i, :],
+                        in0=a_ps[:, i2, :],
+                        scalar=1.0,
+                        in1=bias_all[:],
+                        op0=ALU.mult,
+                        op1=ALU.add,
+                        accum_out=row_sum[:, i : i + 1],
+                    )
+
+            neg_mean = stats.tile([P, GROUP], F32)
+            nc.vector.tensor_scalar_mul(out=neg_mean[:], in0=row_sum[:], scalar1=-1.0 / FEAT)
+            squares = work.tile([P, GROUP, FEAT], F32)
+            sum_sq = stats.tile([P, GROUP], F32)
+            for i in range(GROUP):
+                nc.scalar.activation(
+                    out=squares[:, i, :],
+                    in_=o[:, i, :],
+                    func=ACT.Square,
+                    bias=neg_mean[:, i : i + 1],
+                    accum_out=sum_sq[:, i : i + 1],
+                )
+            std = stats.tile([P, GROUP], F32)
+            nc.scalar.activation(
+                out=std[:], in_=sum_sq[:], func=ACT.Sqrt, scale=1.0 / FEAT, bias=eps[:]
+            )
+            rstd = stats.tile([P, GROUP], F32)
+            nc.vector.reciprocal(out=rstd[:], in_=std[:])
+
+            t = work.tile([P, GROUP, FEAT], F32)
+            for i in range(GROUP):
+                nc.vector.tensor_scalar(
+                    out=t[:, i, :],
+                    in0=o[:, i, :],
+                    scalar1=neg_mean[:, i : i + 1],
+                    scalar2=rstd[:, i : i + 1],
+                    op0=ALU.add,
+                    op1=ALU.mult,
+                )
+
+            yT = work.tile([P, HALVES, GROUP * P], F32)
+            for j in range(HALVES):
+                tT_ps = psum.tile([P, GROUP * P], F32)
+                for i in range(GROUP):
+                    nc.tensor.transpose(
+                        tT_ps[:, i * P : (i + 1) * P], t[:, i, j * P : (j + 1) * P], ident[:]
+                    )
+                nc.scalar.activation(
+                    out=yT[:, j, :],
+                    in_=tT_ps[:],
+                    func=ACT.Identity,
+                    scale=norm_cols[:, j : j + 1],
+                    bias=norm_cols[:, HALVES + j : HALVES + j + 1],
+                )
+
+            result = work.tile([P, GROUP * FEAT], F32)
+            for pair in range(GROUP // PAIR):
+                y_ps = psum.tile([P, PAIR, FEAT], F32)
+                for i2 in range(PAIR):
+                    i = pair * PAIR + i2
+                    for j in range(HALVES):
+                        nc.tensor.transpose(
+                            y_ps[:, i2, j * P : (j + 1) * P], yT[:, j, i * P : (i + 1) * P], ident[:]
+                        )
+                cols = slice(pair * PAIR * FEAT, (pair + 1) * PAIR * FEAT)
+                nc.vector.tensor_tensor(
+                    out=result[:, cols],
+                    in0=y_ps[:].rearrange("p i n -> p (i n)"),
+                    in1=x_tiles[g][:, cols],
+                    op=ALU.add,
+                )
+            nc.sync.dma_start(
+                out=out_rows[:, g * GROUP : (g + 1) * GROUP, :],
+                in_=result[:].rearrange("p (i n) -> p i n", i=GROUP),
+            )

@@ -105,10 +105,21 @@ def tile_dcadecoderblock_pb_t_kernel(
         norm_cols = consts.tile([P, 2 * HALVES], F32)
         nc.vector.tensor_copy(out=norm_cols[:], in_=norm_ps[:, 0 : 2 * HALVES])
 
-        for g in range(GROUPS):
+        grouped_of = {}
+        hT_of = {}
+        codes_of = {}
+        a_of = {}
+        o_of = {}
+        mean_of = {}
+        std_of = {}
+        t_of = {}
+        tT_of = {}
+        yT_of = {}
+        y_of = {}
+
+        def transpose_h(g):
             h_words = h_tiles[g][:].bitcast(F32)
-            grouped = work.tile([P, GROUP * P * PACK], BF16, align_bytes=64)
-            grouped_words = grouped[:].bitcast(F32)
+            hT_of[g] = []
             for pair in range(GROUP // PAIR):
                 hT_ps = psum.tile([P, PAIR * WORDS], F32)
                 for c in range(PAIR * WORDS // P):
@@ -116,21 +127,31 @@ def tile_dcadecoderblock_pb_t_kernel(
                     nc.tensor.transpose(
                         hT_ps[:, c * P : (c + 1) * P], h_words[:, src : src + P], ident[:]
                     )
+                hT_of[g].append(hT_ps)
+
+        def regroup_h(g):
+            grouped = work.tile([P, GROUP * P * PACK], BF16, align_bytes=64)
+            grouped_words = grouped[:].bitcast(F32)
+            for pair in range(GROUP // PAIR):
                 nc.scalar.copy(
                     out=grouped_words[:, pair * PAIR * WORDS : (pair + 1) * PAIR * WORDS].rearrange(
                         "p (i r u) -> p i r u", i=PAIR, u=2
                     ),
-                    in_=hT_ps[:].rearrange("p (i u r) -> p i r u", i=PAIR, u=2),
+                    in_=hT_of[g][pair][:].rearrange("p (i u r) -> p i r u", i=PAIR, u=2),
                 )
+            grouped_of[g] = grouped
 
+        def quantise_h(g):
             h_codes = work.tile([P, GROUP * P], U32, align_bytes=64)
             h_scales = work.tile([P, GROUP * P], U8, align_bytes=64)
             nc.vector.quantize_mx(
-                out=h_codes[:].bitcast(FP8X4), scales=h_scales[:], in_=grouped[:]
+                out=h_codes[:].bitcast(FP8X4), scales=h_scales[:], in_=grouped_of[g][:]
             )
+            codes_of[g] = (h_codes, h_scales)
 
-            o = work.tile([P, GROUP, FEAT], F32)
-            row_sum = stats.tile([P, GROUP], F32)
+        def project(g):
+            h_codes, h_scales = codes_of[g]
+            a_of[g] = []
             for pair in range(GROUP // PAIR):
                 a_ps = psum.tile([P, PAIR, FEAT], F32)
                 for i2 in range(PAIR):
@@ -144,76 +165,101 @@ def tile_dcadecoderblock_pb_t_kernel(
                         start=True,
                         stop=True,
                     )
-                for i2 in range(PAIR):
-                    i = pair * PAIR + i2
-                    nc.vector.scalar_tensor_tensor(
-                        out=o[:, i, :],
-                        in0=a_ps[:, i2, :],
-                        scalar=1.0,
-                        in1=bias_all[:],
-                        op0=ALU.mult,
-                        op1=ALU.add,
-                        accum_out=row_sum[:, i : i + 1],
-                    )
+                a_of[g].append(a_ps)
 
+        def add_bias(g):
+            o = work.tile([P, GROUP, FEAT], F32)
+            row_sum = stats.tile([P, GROUP], F32)
+            for i in range(GROUP):
+                nc.vector.scalar_tensor_tensor(
+                    out=o[:, i, :],
+                    in0=a_of[g][i // PAIR][:, i % PAIR, :],
+                    scalar=1.0,
+                    in1=bias_all[:],
+                    op0=ALU.mult,
+                    op1=ALU.add,
+                    accum_out=row_sum[:, i : i + 1],
+                )
             neg_mean = stats.tile([P, GROUP], F32)
             nc.vector.tensor_scalar_mul(out=neg_mean[:], in0=row_sum[:], scalar1=-1.0 / FEAT)
+            o_of[g] = o
+            mean_of[g] = neg_mean
+
+        def deviation(g):
             squares = work.tile([P, GROUP, FEAT], F32)
             sum_sq = stats.tile([P, GROUP], F32)
             for i in range(GROUP):
                 nc.scalar.activation(
                     out=squares[:, i, :],
-                    in_=o[:, i, :],
+                    in_=o_of[g][:, i, :],
                     func=ACT.Square,
-                    bias=neg_mean[:, i : i + 1],
+                    bias=mean_of[g][:, i : i + 1],
                     accum_out=sum_sq[:, i : i + 1],
                 )
             std = stats.tile([P, GROUP], F32)
             nc.scalar.activation(
                 out=std[:], in_=sum_sq[:], func=ACT.Sqrt, scale=1.0 / FEAT, bias=eps[:]
             )
-            rstd = stats.tile([P, GROUP], F32)
-            nc.vector.reciprocal(out=rstd[:], in_=std[:])
+            std_of[g] = std
 
+        def normalise(g):
+            rstd = stats.tile([P, GROUP], F32)
+            nc.vector.reciprocal(out=rstd[:], in_=std_of[g][:])
             t = work.tile([P, GROUP, FEAT], F32)
             for i in range(GROUP):
                 nc.vector.tensor_scalar(
                     out=t[:, i, :],
-                    in0=o[:, i, :],
-                    scalar1=neg_mean[:, i : i + 1],
+                    in0=o_of[g][:, i, :],
+                    scalar1=mean_of[g][:, i : i + 1],
                     scalar2=rstd[:, i : i + 1],
                     op0=ALU.add,
                     op1=ALU.mult,
                 )
+            t_of[g] = t
 
-            yT = work.tile([P, HALVES, GROUP * P], F32)
+        def features_to_partitions(g):
+            tT_of[g] = []
             for j in range(HALVES):
                 tT_ps = psum.tile([P, GROUP * P], F32)
                 for i in range(GROUP):
                     nc.tensor.transpose(
-                        tT_ps[:, i * P : (i + 1) * P], t[:, i, j * P : (j + 1) * P], ident[:]
+                        tT_ps[:, i * P : (i + 1) * P], t_of[g][:, i, j * P : (j + 1) * P], ident[:]
                     )
+                tT_of[g].append(tT_ps)
+
+        def gain_and_shift(g):
+            yT = work.tile([P, HALVES, GROUP * P], F32)
+            for j in range(HALVES):
                 nc.scalar.activation(
                     out=yT[:, j, :],
-                    in_=tT_ps[:],
+                    in_=tT_of[g][j][:],
                     func=ACT.Identity,
                     scale=norm_cols[:, j : j + 1],
                     bias=norm_cols[:, HALVES + j : HALVES + j + 1],
                 )
+            yT_of[g] = yT
 
-            result = work.tile([P, GROUP * FEAT], F32)
+        def rows_to_partitions(g):
+            y_of[g] = []
             for pair in range(GROUP // PAIR):
                 y_ps = psum.tile([P, PAIR, FEAT], F32)
                 for i2 in range(PAIR):
                     i = pair * PAIR + i2
                     for j in range(HALVES):
                         nc.tensor.transpose(
-                            y_ps[:, i2, j * P : (j + 1) * P], yT[:, j, i * P : (i + 1) * P], ident[:]
+                            y_ps[:, i2, j * P : (j + 1) * P],
+                            yT_of[g][:, j, i * P : (i + 1) * P],
+                            ident[:],
                         )
+                y_of[g].append(y_ps)
+
+        def add_residual_and_store(g):
+            result = work.tile([P, GROUP * FEAT], F32)
+            for pair in range(GROUP // PAIR):
                 cols = slice(pair * PAIR * FEAT, (pair + 1) * PAIR * FEAT)
                 nc.vector.tensor_tensor(
                     out=result[:, cols],
-                    in0=y_ps[:].rearrange("p i n -> p (i n)"),
+                    in0=y_of[g][pair][:].rearrange("p i n -> p (i n)"),
                     in1=x_tiles[g][:, cols],
                     op=ALU.add,
                 )
@@ -221,3 +267,31 @@ def tile_dcadecoderblock_pb_t_kernel(
                 out=out_rows[:, g * GROUP : (g + 1) * GROUP, :],
                 in_=result[:].rearrange("p (i n) -> p i n", i=GROUP),
             )
+
+        def in_range(g):
+            return 0 <= g < GROUPS
+
+        with tc.manual_schedule():
+            for s in range(GROUPS + 4):
+                if in_range(s - 1):
+                    quantise_h(s - 1)
+                if in_range(s - 4):
+                    rows_to_partitions(s - 4)
+                if in_range(s - 3):
+                    features_to_partitions(s - 3)
+                if in_range(s):
+                    transpose_h(s)
+                if in_range(s - 1):
+                    project(s - 1)
+                if in_range(s - 2):
+                    deviation(s - 2)
+                if in_range(s - 3):
+                    gain_and_shift(s - 3)
+                if in_range(s):
+                    regroup_h(s)
+                if in_range(s - 4):
+                    add_residual_and_store(s - 4)
+                if in_range(s - 2):
+                    normalise(s - 2)
+                if in_range(s - 1):
+                    add_bias(s - 1)

@@ -23,6 +23,7 @@ GROUP = 4
 PAIR = 2
 GROUPS = TILES // GROUP
 EPS = 1e-5
+MX_REPEAT = 2
 
 FLOPS = 2 * ROWS * K * FEAT
 
@@ -149,13 +150,12 @@ def tile_dcadecoderblock_pb_t_kernel(
             )
             codes_of[g] = (h_codes, h_scales)
 
-        def project(g):
+        def project(g, pair):
             h_codes, h_scales = codes_of[g]
-            a_of[g] = []
-            for pair in range(GROUP // PAIR):
-                a_ps = psum.tile([P, PAIR, FEAT], F32)
-                for i2 in range(PAIR):
-                    rows = slice((pair * PAIR + i2) * P, (pair * PAIR + i2 + 1) * P)
+            a_ps = psum.tile([P, PAIR, FEAT], F32)
+            for i2 in range(PAIR):
+                rows = slice((pair * PAIR + i2) * P, (pair * PAIR + i2 + 1) * P)
+                for again in range(MX_REPEAT):
                     nc.tensor.matmul_mx(
                         out=a_ps[:, i2, :],
                         lhsT=h_codes[:, rows].bitcast(FP8X4),
@@ -165,7 +165,7 @@ def tile_dcadecoderblock_pb_t_kernel(
                         start=True,
                         stop=True,
                     )
-                a_of[g].append(a_ps)
+            a_of[(g, pair)] = a_ps
 
         def add_bias(g):
             o = work.tile([P, GROUP, FEAT], F32)
@@ -173,7 +173,7 @@ def tile_dcadecoderblock_pb_t_kernel(
             for i in range(GROUP):
                 nc.vector.scalar_tensor_tensor(
                     out=o[:, i, :],
-                    in0=a_of[g][i // PAIR][:, i % PAIR, :],
+                    in0=a_of[(g, i // PAIR)][:, i % PAIR, :],
                     scalar=1.0,
                     in1=bias_all[:],
                     op0=ALU.mult,
@@ -277,12 +277,14 @@ def tile_dcadecoderblock_pb_t_kernel(
                     quantise_h(s - 1)
                 if in_range(s - 4):
                     rows_to_partitions(s - 4)
+                if in_range(s - 1):
+                    project(s - 1, 0)
                 if in_range(s - 3):
                     features_to_partitions(s - 3)
                 if in_range(s):
                     transpose_h(s)
                 if in_range(s - 1):
-                    project(s - 1)
+                    project(s - 1, 1)
                 if in_range(s - 2):
                     deviation(s - 2)
                 if in_range(s - 3):

@@ -19,11 +19,10 @@ FEAT = 256
 HALVES = FEAT // P
 WORDS = K // 2
 TILES = ROWS // P
-GROUP = 4
 PAIR = 2
-GROUPS = TILES // GROUP
+PAIRS = TILES // PAIR
+CHUNK = 4
 EPS = 1e-5
-MX_REPEAT = 2
 
 FLOPS = 2 * ROWS * K * FEAT
 
@@ -38,39 +37,53 @@ def tile_dcadecoderblock_pb_t_kernel(
 
     with ExitStack() as stack:
         consts = stack.enter_context(tc.tile_pool(name="consts", bufs=1))
-        loads = stack.enter_context(tc.tile_pool(name="loads", bufs=GROUPS))
+        loads = stack.enter_context(tc.tile_pool(name="loads", bufs=TILES // CHUNK))
         work = stack.enter_context(tc.tile_pool(name="work", bufs=3))
-        stats = stack.enter_context(tc.tile_pool(name="stats", bufs=4))
+        long_lived = stack.enter_context(tc.tile_pool(name="long_lived", bufs=7))
         psum = stack.enter_context(tc.psum_pool(name="psum", bufs=2))
-
-        h_tiles = []
-        x_tiles = []
-        for g in range(GROUPS):
-            tiles = slice(g * GROUP, (g + 1) * GROUP)
-            h_sb = loads.tile([P, GROUP * K], BF16)
-            nc.sync.dma_start(
-                out=h_sb[:].rearrange("p (i k) -> p i k", i=GROUP), in_=h_rows[:, tiles, :]
-            )
-            h_tiles.append(h_sb)
-            x_sb = loads.tile([P, GROUP * FEAT], BF16)
-            nc.sync.dma_start(
-                out=x_sb[:].rearrange("p (i n) -> p i n", i=GROUP), in_=x_rows[:, tiles, :]
-            )
-            x_tiles.append(x_sb)
-
-        eps = consts.tile([P, 1], F32)
-        nc.vector.memset(eps[:], EPS)
-        table_warm = consts.tile([P, 1], F32)
-        nc.scalar.activation(out=table_warm[:], in_=eps[:], func=ACT.Sqrt)
+        stack.enter_context(tc.manual_schedule())
 
         ident = consts.tile([P, P], F32)
         make_identity(nc, ident[:])
 
         w_raw = consts.tile([P, PACK, FEAT], BF16)
         nc.scalar.dma_start(
-            out=w_raw[:].rearrange("p (u e) n -> p u e n", u=2),
-            in_=attn_out_W.rearrange("(u p e) n -> p u e n", u=2, e=2),
+            out=w_raw[:].rearrange("p (v e) n -> p v e n", v=2),
+            in_=attn_out_W.rearrange("(v p e) n -> p v e n", v=2, e=2),
         )
+        bias_row = consts.tile([P, FEAT], BF16)
+        nc.vector.memset(bias_row[:], 0.0)
+        nc.scalar.dma_start(out=bias_row[0:1, :], in_=attn_out_b.rearrange("(o n) -> o n", o=1))
+        norm_rows = consts.tile([P, P], BF16)
+        nc.vector.memset(norm_rows[:], 0.0)
+        nc.scalar.dma_start(
+            out=norm_rows[0:HALVES, :], in_=attn_norm_g.rearrange("(j p) -> j p", p=P)
+        )
+        nc.scalar.dma_start(
+            out=norm_rows[HALVES : 2 * HALVES, :], in_=attn_norm_b.rearrange("(j p) -> j p", p=P)
+        )
+        ones = consts.tile([P, P], BF16)
+        nc.vector.memset(ones[:], 1.0)
+        eps = consts.tile([P, 1], F32)
+        nc.vector.memset(eps[:], EPS)
+        table_warm = consts.tile([P, 1], F32)
+        nc.scalar.activation(out=table_warm[:], in_=eps[:], func=ACT.Sqrt)
+
+        h_chunks = []
+        x_chunks = []
+        for c in range(TILES // CHUNK):
+            tiles = slice(c * CHUNK, (c + 1) * CHUNK)
+            h_sb = loads.tile([P, CHUNK * K], BF16)
+            nc.sync.dma_start(
+                out=h_sb[:].rearrange("p (i k) -> p i k", i=CHUNK), in_=h_rows[:, tiles, :]
+            )
+            h_chunks.append(h_sb)
+            x_sb = loads.tile([P, CHUNK * FEAT], BF16)
+            nc.sync.dma_start(
+                out=x_sb[:].rearrange("p (i n) -> p i n", i=CHUNK), in_=x_rows[:, tiles, :]
+            )
+            x_chunks.append(x_sb)
+
         w_grouped = consts.tile([P, FEAT, PACK], BF16, align_bytes=64)
         nc.vector.tensor_copy(out=w_grouped[:], in_=w_raw[:].rearrange("p t n -> p n t"))
         w_codes = consts.tile([P, FEAT], U32, align_bytes=64)
@@ -80,220 +93,198 @@ def tile_dcadecoderblock_pb_t_kernel(
             scales=w_scales[:],
             in_=w_grouped[:].rearrange("p n t -> p (n t)"),
         )
-
-        ones = consts.tile([P, P], BF16)
-        nc.vector.memset(ones[:], 1.0)
-        bias_row = consts.tile([P, FEAT], BF16)
-        nc.vector.memset(bias_row[:], 0.0)
-        nc.scalar.dma_start(out=bias_row[0:1, :], in_=attn_out_b.rearrange("(o n) -> o n", o=1))
-        bias_ps = psum.tile([P, FEAT], F32, tag="a_ps")
-        nc.tensor.matmul(out=bias_ps[:], lhsT=ones[:], rhs=bias_row[:], start=True, stop=True)
-        bias_all = consts.tile([P, FEAT], F32)
-        nc.vector.tensor_copy(out=bias_all[:], in_=bias_ps[:])
-
-        norm_rows = consts.tile([P, P], BF16)
-        nc.vector.memset(norm_rows[:], 0.0)
-        nc.scalar.dma_start(
-            out=norm_rows[0:HALVES, :], in_=attn_norm_g.rearrange("(j p) -> j p", p=P)
-        )
-        nc.scalar.dma_start(
-            out=norm_rows[HALVES : 2 * HALVES, :], in_=attn_norm_b.rearrange("(j p) -> j p", p=P)
-        )
         norm_rows_f32 = consts.tile([P, P], F32)
         nc.vector.tensor_copy(out=norm_rows_f32[:], in_=norm_rows[:])
-        norm_ps = psum.tile([P, P], F32, tag="tT_ps")
-        nc.tensor.transpose(norm_ps[:], norm_rows_f32[:], ident[:])
+        bias_all = consts.tile([P, FEAT], F32)
         norm_cols = consts.tile([P, 2 * HALVES], F32)
-        nc.vector.tensor_copy(out=norm_cols[:], in_=norm_ps[:, 0 : 2 * HALVES])
 
-        grouped_of = {}
-        hT_of = {}
-        codes_of = {}
-        a_of = {}
-        o_of = {}
-        mean_of = {}
-        std_of = {}
-        t_of = {}
-        tT_of = {}
-        yT_of = {}
-        y_of = {}
+        def spread_constants():
+            bias_ps = psum.tile([P, FEAT], F32, tag="a_ps")
+            nc.tensor.matmul(out=bias_ps[:], lhsT=ones[:], rhs=bias_row[:], start=True, stop=True)
+            nc.vector.tensor_copy(out=bias_all[:], in_=bias_ps[:])
+            norm_ps = psum.tile([P, P], F32, tag="tT_ps")
+            nc.tensor.transpose(norm_ps[:], norm_rows_f32[:], ident[:])
+            nc.vector.tensor_copy(out=norm_cols[:], in_=norm_ps[:, 0 : 2 * HALVES])
 
-        def transpose_h(g):
-            h_words = h_tiles[g][:].bitcast(F32)
-            hT_of[g] = []
-            for pair in range(GROUP // PAIR):
-                hT_ps = psum.tile([P, PAIR * WORDS], F32)
-                for c in range(PAIR * WORDS // P):
-                    src = pair * PAIR * WORDS + c * P
-                    nc.tensor.transpose(
-                        hT_ps[:, c * P : (c + 1) * P], h_words[:, src : src + P], ident[:]
-                    )
-                hT_of[g].append(hT_ps)
+        kept = {}
 
-        def regroup_h(g):
-            grouped = work.tile([P, GROUP * P * PACK], BF16, align_bytes=64)
-            grouped_words = grouped[:].bitcast(F32)
-            for pair in range(GROUP // PAIR):
-                nc.scalar.copy(
-                    out=grouped_words[:, pair * PAIR * WORDS : (pair + 1) * PAIR * WORDS].rearrange(
-                        "p (i r u) -> p i r u", i=PAIR, u=2
-                    ),
-                    in_=hT_of[g][pair][:].rearrange("p (i u r) -> p i r u", i=PAIR, u=2),
+        def transpose_h(u):
+            first = (u * PAIR % CHUNK) * WORDS
+            h_words = h_chunks[u * PAIR // CHUNK][:].bitcast(F32)
+            hT_ps = psum.tile([P, PAIR * WORDS], F32)
+            for c in range(PAIR * WORDS // P):
+                nc.tensor.transpose(
+                    hT_ps[:, c * P : (c + 1) * P],
+                    h_words[:, first + c * P : first + (c + 1) * P],
+                    ident[:],
                 )
-            grouped_of[g] = grouped
+            kept["hT", u] = hT_ps
 
-        def quantise_h(g):
-            h_codes = work.tile([P, GROUP * P], U32, align_bytes=64)
-            h_scales = work.tile([P, GROUP * P], U8, align_bytes=64)
-            nc.vector.quantize_mx(
-                out=h_codes[:].bitcast(FP8X4), scales=h_scales[:], in_=grouped_of[g][:]
+        def regroup_h(u):
+            grouped = work.tile([P, PAIR * P * PACK], BF16, align_bytes=64)
+            nc.scalar.copy(
+                out=grouped[:].bitcast(F32).rearrange("p (i r v) -> p i r v", i=PAIR, v=2),
+                in_=kept["hT", u][:].rearrange("p (i v r) -> p i r v", i=PAIR, v=2),
             )
-            codes_of[g] = (h_codes, h_scales)
+            kept["grouped", u] = grouped
 
-        def project(g, pair):
-            h_codes, h_scales = codes_of[g]
+        def quantise_h(u):
+            h_codes = work.tile([P, PAIR * P], U32, align_bytes=64)
+            h_scales = work.tile([P, PAIR * P], U8, align_bytes=64)
+            nc.vector.quantize_mx(
+                out=h_codes[:].bitcast(FP8X4), scales=h_scales[:], in_=kept["grouped", u][:]
+            )
+            kept["codes", u] = h_codes
+            kept["scales", u] = h_scales
+
+        def project(u):
             a_ps = psum.tile([P, PAIR, FEAT], F32)
-            for i2 in range(PAIR):
-                rows = slice((pair * PAIR + i2) * P, (pair * PAIR + i2 + 1) * P)
-                for again in range(MX_REPEAT):
-                    nc.tensor.matmul_mx(
-                        out=a_ps[:, i2, :],
-                        lhsT=h_codes[:, rows].bitcast(FP8X4),
-                        lhsT_scale=h_scales[:, rows],
-                        rhs=w_codes[:].bitcast(FP8X4),
-                        rhs_scale=w_scales[:],
-                        start=True,
-                        stop=True,
-                    )
-            a_of[(g, pair)] = a_ps
+            for i in range(PAIR):
+                nc.tensor.matmul_mx(
+                    out=a_ps[:, i, :],
+                    lhsT=kept["codes", u][:, i * P : (i + 1) * P].bitcast(FP8X4),
+                    lhsT_scale=kept["scales", u][:, i * P : (i + 1) * P],
+                    rhs=w_codes[:].bitcast(FP8X4),
+                    rhs_scale=w_scales[:],
+                    start=True,
+                    stop=True,
+                )
+            kept["a", u] = a_ps
 
-        def add_bias(g):
-            o = work.tile([P, GROUP, FEAT], F32)
-            row_sum = stats.tile([P, GROUP], F32)
-            for i in range(GROUP):
+        def add_bias(u):
+            o = long_lived.tile([P, PAIR, FEAT], F32)
+            row_sum = work.tile([P, PAIR], F32)
+            for i in range(PAIR):
                 nc.vector.scalar_tensor_tensor(
                     out=o[:, i, :],
-                    in0=a_of[(g, i // PAIR)][:, i % PAIR, :],
+                    in0=kept["a", u][:, i, :],
                     scalar=1.0,
                     in1=bias_all[:],
                     op0=ALU.mult,
                     op1=ALU.add,
                     accum_out=row_sum[:, i : i + 1],
                 )
-            neg_mean = stats.tile([P, GROUP], F32)
-            nc.vector.tensor_scalar_mul(out=neg_mean[:], in0=row_sum[:], scalar1=-1.0 / FEAT)
-            o_of[g] = o
-            mean_of[g] = neg_mean
+            kept["o", u] = o
+            kept["row_sum", u] = row_sum
 
-        def deviation(g):
-            squares = work.tile([P, GROUP, FEAT], F32)
-            sum_sq = stats.tile([P, GROUP], F32)
-            for i in range(GROUP):
+        def negate_mean(u):
+            neg_mean = long_lived.tile([P, PAIR], F32)
+            nc.vector.tensor_scalar_mul(
+                out=neg_mean[:], in0=kept["row_sum", u][:], scalar1=-1.0 / FEAT
+            )
+            kept["neg_mean", u] = neg_mean
+
+        def sum_squares(u):
+            squares = work.tile([P, PAIR, FEAT], F32)
+            sum_sq = work.tile([P, PAIR], F32)
+            for i in range(PAIR):
                 nc.scalar.activation(
                     out=squares[:, i, :],
-                    in_=o_of[g][:, i, :],
+                    in_=kept["o", u][:, i, :],
                     func=ACT.Square,
-                    bias=mean_of[g][:, i : i + 1],
+                    bias=kept["neg_mean", u][:, i : i + 1],
                     accum_out=sum_sq[:, i : i + 1],
                 )
-            std = stats.tile([P, GROUP], F32)
-            nc.scalar.activation(
-                out=std[:], in_=sum_sq[:], func=ACT.Sqrt, scale=1.0 / FEAT, bias=eps[:]
-            )
-            std_of[g] = std
+            kept["sum_sq", u] = sum_sq
 
-        def normalise(g):
-            rstd = stats.tile([P, GROUP], F32)
-            nc.vector.reciprocal(out=rstd[:], in_=std_of[g][:])
-            t = work.tile([P, GROUP, FEAT], F32)
-            for i in range(GROUP):
+        def root(u):
+            std = work.tile([P, PAIR], F32)
+            nc.scalar.activation(
+                out=std[:], in_=kept["sum_sq", u][:], func=ACT.Sqrt, scale=1.0 / FEAT, bias=eps[:]
+            )
+            kept["std", u] = std
+
+        def invert(u):
+            rstd = work.tile([P, PAIR], F32)
+            nc.vector.reciprocal(out=rstd[:], in_=kept["std", u][:])
+            kept["rstd", u] = rstd
+
+        def normalise(u):
+            t = work.tile([P, PAIR, FEAT], F32)
+            for i in range(PAIR):
                 nc.vector.tensor_scalar(
                     out=t[:, i, :],
-                    in0=o_of[g][:, i, :],
-                    scalar1=mean_of[g][:, i : i + 1],
-                    scalar2=rstd[:, i : i + 1],
+                    in0=kept["o", u][:, i, :],
+                    scalar1=kept["neg_mean", u][:, i : i + 1],
+                    scalar2=kept["rstd", u][:, i : i + 1],
                     op0=ALU.add,
                     op1=ALU.mult,
                 )
-            t_of[g] = t
+            kept["t", u] = t
 
-        def features_to_partitions(g):
-            tT_of[g] = []
+        def features_to_partitions(u):
+            tT_ps = psum.tile([P, HALVES, PAIR * P], F32)
             for j in range(HALVES):
-                tT_ps = psum.tile([P, GROUP * P], F32)
-                for i in range(GROUP):
+                for i in range(PAIR):
                     nc.tensor.transpose(
-                        tT_ps[:, i * P : (i + 1) * P], t_of[g][:, i, j * P : (j + 1) * P], ident[:]
+                        tT_ps[:, j, i * P : (i + 1) * P],
+                        kept["t", u][:, i, j * P : (j + 1) * P],
+                        ident[:],
                     )
-                tT_of[g].append(tT_ps)
+            kept["tT", u] = tT_ps
 
-        def gain_and_shift(g):
-            yT = work.tile([P, HALVES, GROUP * P], F32)
+        def gain_and_shift(u):
+            yT = work.tile([P, HALVES, PAIR * P], F32)
             for j in range(HALVES):
                 nc.scalar.activation(
                     out=yT[:, j, :],
-                    in_=tT_of[g][j][:],
+                    in_=kept["tT", u][:, j, :],
                     func=ACT.Identity,
                     scale=norm_cols[:, j : j + 1],
                     bias=norm_cols[:, HALVES + j : HALVES + j + 1],
                 )
-            yT_of[g] = yT
+            kept["yT", u] = yT
 
-        def rows_to_partitions(g):
-            y_of[g] = []
-            for pair in range(GROUP // PAIR):
-                y_ps = psum.tile([P, PAIR, FEAT], F32)
-                for i2 in range(PAIR):
-                    i = pair * PAIR + i2
-                    for j in range(HALVES):
-                        nc.tensor.transpose(
-                            y_ps[:, i2, j * P : (j + 1) * P],
-                            yT_of[g][:, j, i * P : (i + 1) * P],
-                            ident[:],
-                        )
-                y_of[g].append(y_ps)
+        def rows_to_partitions(u):
+            y_ps = psum.tile([P, PAIR, FEAT], F32)
+            for i in range(PAIR):
+                for j in range(HALVES):
+                    nc.tensor.transpose(
+                        y_ps[:, i, j * P : (j + 1) * P],
+                        kept["yT", u][:, j, i * P : (i + 1) * P],
+                        ident[:],
+                    )
+            kept["y", u] = y_ps
 
-        def add_residual_and_store(g):
-            result = work.tile([P, GROUP * FEAT], F32)
-            for pair in range(GROUP // PAIR):
-                cols = slice(pair * PAIR * FEAT, (pair + 1) * PAIR * FEAT)
-                nc.vector.tensor_tensor(
-                    out=result[:, cols],
-                    in0=y_of[g][pair][:].rearrange("p i n -> p (i n)"),
-                    in1=x_tiles[g][:, cols],
-                    op=ALU.add,
-                )
+        def add_residual_and_store(u):
+            first = (u * PAIR % CHUNK) * FEAT
+            result = work.tile([P, PAIR * FEAT], F32)
+            nc.vector.tensor_tensor(
+                out=result[:],
+                in0=kept["y", u][:].rearrange("p i n -> p (i n)"),
+                in1=x_chunks[u * PAIR // CHUNK][:, first : first + PAIR * FEAT],
+                op=ALU.add,
+            )
             nc.sync.dma_start(
-                out=out_rows[:, g * GROUP : (g + 1) * GROUP, :],
-                in_=result[:].rearrange("p (i n) -> p i n", i=GROUP),
+                out=out_rows[:, u * PAIR : (u + 1) * PAIR, :],
+                in_=result[:].rearrange("p (i n) -> p i n", i=PAIR),
             )
 
-        def in_range(g):
-            return 0 <= g < GROUPS
+        stages = [
+            transpose_h,
+            regroup_h,
+            quantise_h,
+            project,
+            add_bias,
+            negate_mean,
+            sum_squares,
+            root,
+            invert,
+            normalise,
+            features_to_partitions,
+            gain_and_shift,
+            rows_to_partitions,
+            add_residual_and_store,
+        ]
 
-        with tc.manual_schedule():
-            for s in range(GROUPS + 4):
-                if in_range(s - 1):
-                    quantise_h(s - 1)
-                if in_range(s - 4):
-                    rows_to_partitions(s - 4)
-                if in_range(s - 1):
-                    project(s - 1, 0)
-                if in_range(s - 3):
-                    features_to_partitions(s - 3)
-                if in_range(s):
-                    transpose_h(s)
-                if in_range(s - 1):
-                    project(s - 1, 1)
-                if in_range(s - 2):
-                    deviation(s - 2)
-                if in_range(s - 3):
-                    gain_and_shift(s - 3)
-                if in_range(s):
-                    regroup_h(s)
-                if in_range(s - 4):
-                    add_residual_and_store(s - 4)
-                if in_range(s - 2):
-                    normalise(s - 2)
-                if in_range(s - 1):
-                    add_bias(s - 1)
+        def one_round(s):
+            for n, stage in reversed(list(enumerate(stages))):
+                if 0 <= s - n < PAIRS:
+                    stage(s - n)
+
+        first_product = stages.index(project)
+        for s in range(first_product):
+            one_round(s)
+        spread_constants()
+        for s in range(first_product, PAIRS + len(stages) - 1):
+            one_round(s)

@@ -23,6 +23,7 @@ PAIR = 2
 PAIRS = TILES // PAIR
 CHUNK = 4
 EPS = 1e-5
+MX_REPEAT = 2
 
 FLOPS = 2 * ROWS * K * FEAT
 
@@ -140,15 +141,16 @@ def tile_dcadecoderblock_pb_t_kernel(
         def project(u):
             a_ps = psum.tile([P, PAIR, FEAT], F32)
             for i in range(PAIR):
-                nc.tensor.matmul_mx(
-                    out=a_ps[:, i, :],
-                    lhsT=kept["codes", u][:, i * P : (i + 1) * P].bitcast(FP8X4),
-                    lhsT_scale=kept["scales", u][:, i * P : (i + 1) * P],
-                    rhs=w_codes[:].bitcast(FP8X4),
-                    rhs_scale=w_scales[:],
-                    start=True,
-                    stop=True,
-                )
+                for again in range(MX_REPEAT):
+                    nc.tensor.matmul_mx(
+                        out=a_ps[:, i, :],
+                        lhsT=kept["codes", u][:, i * P : (i + 1) * P].bitcast(FP8X4),
+                        lhsT_scale=kept["scales", u][:, i * P : (i + 1) * P],
+                        rhs=w_codes[:].bitcast(FP8X4),
+                        rhs_scale=w_scales[:],
+                        start=True,
+                        stop=True,
+                    )
             kept["a", u] = a_ps
 
         def add_bias(u):

@@ -23,7 +23,6 @@ PAIR = 2
 PAIRS = TILES // PAIR
 CHUNK = 4
 EPS = 1e-5
-MX_REPEAT = 2
 
 FLOPS = 2 * ROWS * K * FEAT
 
@@ -141,16 +140,15 @@ def tile_dcadecoderblock_pb_t_kernel(
         def project(u):
             a_ps = psum.tile([P, PAIR, FEAT], F32)
             for i in range(PAIR):
-                for again in range(MX_REPEAT):
-                    nc.tensor.matmul_mx(
-                        out=a_ps[:, i, :],
-                        lhsT=kept["codes", u][:, i * P : (i + 1) * P].bitcast(FP8X4),
-                        lhsT_scale=kept["scales", u][:, i * P : (i + 1) * P],
-                        rhs=w_codes[:].bitcast(FP8X4),
-                        rhs_scale=w_scales[:],
-                        start=True,
-                        stop=True,
-                    )
+                nc.tensor.matmul_mx(
+                    out=a_ps[:, i, :],
+                    lhsT=kept["codes", u][:, i * P : (i + 1) * P].bitcast(FP8X4),
+                    lhsT_scale=kept["scales", u][:, i * P : (i + 1) * P],
+                    rhs=w_codes[:].bitcast(FP8X4),
+                    rhs_scale=w_scales[:],
+                    start=True,
+                    stop=True,
+                )
             kept["a", u] = a_ps
 
         def add_bias(u):
@@ -204,7 +202,7 @@ def tile_dcadecoderblock_pb_t_kernel(
         def normalise(u):
             t = work.tile([P, PAIR, FEAT], F32)
             for i in range(PAIR):
-                nc.vector.tensor_scalar(
+                nc.gpsimd.tensor_scalar(
                     out=t[:, i, :],
                     in0=kept["o", u][:, i, :],
                     scalar1=kept["neg_mean", u][:, i : i + 1],

@@ -23,6 +23,7 @@ PAIR = 2
 PAIRS = TILES // PAIR
 CHUNK = 4
 EPS = 1e-5
+VECTOR_SHARE = 3
 
 FLOPS = 2 * ROWS * K * FEAT
 
@@ -39,7 +40,8 @@ def tile_dcadecoderblock_pb_t_kernel(
         consts = stack.enter_context(tc.tile_pool(name="consts", bufs=1))
         loads = stack.enter_context(tc.tile_pool(name="loads", bufs=TILES // CHUNK))
         work = stack.enter_context(tc.tile_pool(name="work", bufs=3))
-        long_lived = stack.enter_context(tc.tile_pool(name="long_lived", bufs=7))
+        long_lived = stack.enter_context(tc.tile_pool(name="long_lived", bufs=6))
+        results = stack.enter_context(tc.tile_pool(name="results", bufs=8))
         psum = stack.enter_context(tc.psum_pool(name="psum", bufs=2))
         stack.enter_context(tc.manual_schedule())
 
@@ -67,7 +69,7 @@ def tile_dcadecoderblock_pb_t_kernel(
         eps = consts.tile([P, 1], F32)
         nc.vector.memset(eps[:], EPS)
         table_warm = consts.tile([P, 1], F32)
-        nc.scalar.activation(out=table_warm[:], in_=eps[:], func=ACT.Sqrt)
+        nc.scalar.activation(out=table_warm[:], in_=eps[:], func=ACT.Abs_reciprocal_sqrt)
 
         h_chunks = []
         x_chunks = []
@@ -122,10 +124,12 @@ def tile_dcadecoderblock_pb_t_kernel(
 
         def regroup_h(u):
             grouped = work.tile([P, PAIR * P * PACK], BF16, align_bytes=64)
-            nc.scalar.copy(
-                out=grouped[:].bitcast(F32).rearrange("p (i r v) -> p i r v", i=PAIR, v=2),
-                in_=kept["hT", u][:].rearrange("p (i v r) -> p i r v", i=PAIR, v=2),
-            )
+            side_by_side = grouped[:].bitcast(F32).rearrange("p (i r v) -> p i r v", i=PAIR, v=2)
+            bank = kept["hT", u][:].rearrange("p (i v r) -> p i r v", i=PAIR, v=2)
+            if u % VECTOR_SHARE == VECTOR_SHARE - 1:
+                nc.vector.tensor_copy(out=side_by_side, in_=bank)
+            else:
+                nc.scalar.copy(out=side_by_side, in_=bank)
             kept["grouped", u] = grouped
 
         def quantise_h(u):
@@ -169,8 +173,13 @@ def tile_dcadecoderblock_pb_t_kernel(
 
         def negate_mean(u):
             neg_mean = long_lived.tile([P, PAIR], F32)
-            nc.vector.tensor_scalar_mul(
-                out=neg_mean[:], in0=kept["row_sum", u][:], scalar1=-1.0 / FEAT
+            nc.gpsimd.tensor_scalar(
+                out=neg_mean[:],
+                in0=kept["row_sum", u][:],
+                scalar1=-1.0 / FEAT,
+                scalar2=0.0,
+                op0=ALU.mult,
+                op1=ALU.add,
             )
             kept["neg_mean", u] = neg_mean
 
@@ -187,16 +196,15 @@ def tile_dcadecoderblock_pb_t_kernel(
                 )
             kept["sum_sq", u] = sum_sq
 
-        def root(u):
-            std = work.tile([P, PAIR], F32)
-            nc.scalar.activation(
-                out=std[:], in_=kept["sum_sq", u][:], func=ACT.Sqrt, scale=1.0 / FEAT, bias=eps[:]
-            )
-            kept["std", u] = std
-
-        def invert(u):
+        def inverse_root(u):
             rstd = work.tile([P, PAIR], F32)
-            nc.vector.reciprocal(out=rstd[:], in_=kept["std", u][:])
+            nc.scalar.activation(
+                out=rstd[:],
+                in_=kept["sum_sq", u][:],
+                func=ACT.Abs_reciprocal_sqrt,
+                scale=1.0 / FEAT,
+                bias=eps[:],
+            )
             kept["rstd", u] = rstd
 
         def normalise(u):
@@ -248,7 +256,7 @@ def tile_dcadecoderblock_pb_t_kernel(
 
         def add_residual_and_store(u):
             first = (u * PAIR % CHUNK) * FEAT
-            result = work.tile([P, PAIR * FEAT], F32)
+            result = results.tile([P, PAIR * FEAT], F32)
             nc.vector.tensor_tensor(
                 out=result[:],
                 in0=kept["y", u][:].rearrange("p i n -> p (i n)"),
@@ -268,8 +276,7 @@ def tile_dcadecoderblock_pb_t_kernel(
             add_bias,
             negate_mean,
             sum_squares,
-            root,
-            invert,
+            inverse_root,
             normalise,
             features_to_partitions,
             gain_and_shift,

@@ -23,7 +23,7 @@ PAIR = 2
 PAIRS = TILES // PAIR
 CHUNK = 4
 EPS = 1e-5
-VECTOR_SHARE = 3
+VECTOR_SHARE = 5
 
 FLOPS = 2 * ROWS * K * FEAT
 

from contextlib import ExitStack

import concourse.mybir as mybir
from concourse.masks import make_identity

F32 = mybir.dt.float32
BF16 = mybir.dt.bfloat16
U32 = mybir.dt.uint32
U8 = mybir.dt.uint8
FP8X4 = mybir.dt.float8_e4m3fn_x4
ALU = mybir.AluOpType
ACT = mybir.ActivationFunctionType

P = 128
PACK = 4
ROWS = 4 * 2048
K = 512
FEAT = 256
HALVES = FEAT // P
WORDS = K // 2
TILES = ROWS // P
PAIR = 2
PAIRS = TILES // PAIR
CHUNK = 4
EPS = 1e-5
VECTOR_SHARE = 5

FLOPS = 2 * ROWS * K * FEAT


def tile_dcadecoderblock_pb_t_kernel(
    tc, h_attn, x, attn_out_W, attn_out_b, attn_norm_g, attn_norm_b, out
):
    nc = tc.nc
    h_rows = h_attn.flatten_outer_dims().rearrange("(p j) k -> p j k", j=TILES)
    x_rows = x.flatten_outer_dims().rearrange("(p j) n -> p j n", j=TILES)
    out_rows = out.flatten_outer_dims().rearrange("(p j) n -> p j n", j=TILES)

    with ExitStack() as stack:
        consts = stack.enter_context(tc.tile_pool(name="consts", bufs=1))
        loads = stack.enter_context(tc.tile_pool(name="loads", bufs=TILES // CHUNK))
        work = stack.enter_context(tc.tile_pool(name="work", bufs=3))
        long_lived = stack.enter_context(tc.tile_pool(name="long_lived", bufs=6))
        results = stack.enter_context(tc.tile_pool(name="results", bufs=8))
        psum = stack.enter_context(tc.psum_pool(name="psum", bufs=2))
        stack.enter_context(tc.manual_schedule())

        ident = consts.tile([P, P], F32)
        make_identity(nc, ident[:])

        w_raw = consts.tile([P, PACK, FEAT], BF16)
        nc.scalar.dma_start(
            out=w_raw[:].rearrange("p (v e) n -> p v e n", v=2),
            in_=attn_out_W.rearrange("(v p e) n -> p v e n", v=2, e=2),
        )
        bias_row = consts.tile([P, FEAT], BF16)
        nc.vector.memset(bias_row[:], 0.0)
        nc.scalar.dma_start(out=bias_row[0:1, :], in_=attn_out_b.rearrange("(o n) -> o n", o=1))
        norm_rows = consts.tile([P, P], BF16)
        nc.vector.memset(norm_rows[:], 0.0)
        nc.scalar.dma_start(
            out=norm_rows[0:HALVES, :], in_=attn_norm_g.rearrange("(j p) -> j p", p=P)
        )
        nc.scalar.dma_start(
            out=norm_rows[HALVES : 2 * HALVES, :], in_=attn_norm_b.rearrange("(j p) -> j p", p=P)
        )
        ones = consts.tile([P, P], BF16)
        nc.vector.memset(ones[:], 1.0)
        eps = consts.tile([P, 1], F32)
        nc.vector.memset(eps[:], EPS)
        table_warm = consts.tile([P, 1], F32)
        nc.scalar.activation(out=table_warm[:], in_=eps[:], func=ACT.Abs_reciprocal_sqrt)

        h_chunks = []
        x_chunks = []
        for c in range(TILES // CHUNK):
            tiles = slice(c * CHUNK, (c + 1) * CHUNK)
            h_sb = loads.tile([P, CHUNK * K], BF16)
            nc.sync.dma_start(
                out=h_sb[:].rearrange("p (i k) -> p i k", i=CHUNK), in_=h_rows[:, tiles, :]
            )
            h_chunks.append(h_sb)
            x_sb = loads.tile([P, CHUNK * FEAT], BF16)
            nc.sync.dma_start(
                out=x_sb[:].rearrange("p (i n) -> p i n", i=CHUNK), in_=x_rows[:, tiles, :]
            )
            x_chunks.append(x_sb)

        w_grouped = consts.tile([P, FEAT, PACK], BF16, align_bytes=64)
        nc.vector.tensor_copy(out=w_grouped[:], in_=w_raw[:].rearrange("p t n -> p n t"))
        w_codes = consts.tile([P, FEAT], U32, align_bytes=64)
        w_scales = consts.tile([P, FEAT], U8, align_bytes=64)
        nc.vector.quantize_mx(
            out=w_codes[:].bitcast(FP8X4),
            scales=w_scales[:],
            in_=w_grouped[:].rearrange("p n t -> p (n t)"),
        )
        norm_rows_f32 = consts.tile([P, P], F32)
        nc.vector.tensor_copy(out=norm_rows_f32[:], in_=norm_rows[:])
        bias_all = consts.tile([P, FEAT], F32)
        norm_cols = consts.tile([P, 2 * HALVES], F32)

        def spread_constants():
            bias_ps = psum.tile([P, FEAT], F32, tag="a_ps")
            nc.tensor.matmul(out=bias_ps[:], lhsT=ones[:], rhs=bias_row[:], start=True, stop=True)
            nc.vector.tensor_copy(out=bias_all[:], in_=bias_ps[:])
            norm_ps = psum.tile([P, P], F32, tag="tT_ps")
            nc.tensor.transpose(norm_ps[:], norm_rows_f32[:], ident[:])
            nc.vector.tensor_copy(out=norm_cols[:], in_=norm_ps[:, 0 : 2 * HALVES])

        kept = {}

        def transpose_h(u):
            first = (u * PAIR % CHUNK) * WORDS
            h_words = h_chunks[u * PAIR // CHUNK][:].bitcast(F32)
            hT_ps = psum.tile([P, PAIR * WORDS], F32)
            for c in range(PAIR * WORDS // P):
                nc.tensor.transpose(
                    hT_ps[:, c * P : (c + 1) * P],
                    h_words[:, first + c * P : first + (c + 1) * P],
                    ident[:],
                )
            kept["hT", u] = hT_ps

        def regroup_h(u):
            grouped = work.tile([P, PAIR * P * PACK], BF16, align_bytes=64)
            side_by_side = grouped[:].bitcast(F32).rearrange("p (i r v) -> p i r v", i=PAIR, v=2)
            bank = kept["hT", u][:].rearrange("p (i v r) -> p i r v", i=PAIR, v=2)
            if u % VECTOR_SHARE == VECTOR_SHARE - 1:
                nc.vector.tensor_copy(out=side_by_side, in_=bank)
            else:
                nc.scalar.copy(out=side_by_side, in_=bank)
            kept["grouped", u] = grouped

        def quantise_h(u):
            h_codes = work.tile([P, PAIR * P], U32, align_bytes=64)
            h_scales = work.tile([P, PAIR * P], U8, align_bytes=64)
            nc.vector.quantize_mx(
                out=h_codes[:].bitcast(FP8X4), scales=h_scales[:], in_=kept["grouped", u][:]
            )
            kept["codes", u] = h_codes
            kept["scales", u] = h_scales

        def project(u):
            a_ps = psum.tile([P, PAIR, FEAT], F32)
            for i in range(PAIR):
                nc.tensor.matmul_mx(
                    out=a_ps[:, i, :],
                    lhsT=kept["codes", u][:, i * P : (i + 1) * P].bitcast(FP8X4),
                    lhsT_scale=kept["scales", u][:, i * P : (i + 1) * P],
                    rhs=w_codes[:].bitcast(FP8X4),
                    rhs_scale=w_scales[:],
                    start=True,
                    stop=True,
                )
            kept["a", u] = a_ps

        def add_bias(u):
            o = long_lived.tile([P, PAIR, FEAT], F32)
            row_sum = work.tile([P, PAIR], F32)
            for i in range(PAIR):
                nc.vector.scalar_tensor_tensor(
                    out=o[:, i, :],
                    in0=kept["a", u][:, i, :],
                    scalar=1.0,
                    in1=bias_all[:],
                    op0=ALU.mult,
                    op1=ALU.add,
                    accum_out=row_sum[:, i : i + 1],
                )
            kept["o", u] = o
            kept["row_sum", u] = row_sum

        def negate_mean(u):
            neg_mean = long_lived.tile([P, PAIR], F32)
            nc.gpsimd.tensor_scalar(
                out=neg_mean[:],
                in0=kept["row_sum", u][:],
                scalar1=-1.0 / FEAT,
                scalar2=0.0,
                op0=ALU.mult,
                op1=ALU.add,
            )
            kept["neg_mean", u] = neg_mean

        def sum_squares(u):
            squares = work.tile([P, PAIR, FEAT], F32)
            sum_sq = work.tile([P, PAIR], F32)
            for i in range(PAIR):
                nc.scalar.activation(
                    out=squares[:, i, :],
                    in_=kept["o", u][:, i, :],
                    func=ACT.Square,
                    bias=kept["neg_mean", u][:, i : i + 1],
                    accum_out=sum_sq[:, i : i + 1],
                )
            kept["sum_sq", u] = sum_sq

        def inverse_root(u):
            rstd = work.tile([P, PAIR], F32)
            nc.scalar.activation(
                out=rstd[:],
                in_=kept["sum_sq", u][:],
                func=ACT.Abs_reciprocal_sqrt,
                scale=1.0 / FEAT,
                bias=eps[:],
            )
            kept["rstd", u] = rstd

        def normalise(u):
            t = work.tile([P, PAIR, FEAT], F32)
            for i in range(PAIR):
                nc.gpsimd.tensor_scalar(
                    out=t[:, i, :],
                    in0=kept["o", u][:, i, :],
                    scalar1=kept["neg_mean", u][:, i : i + 1],
                    scalar2=kept["rstd", u][:, i : i + 1],
                    op0=ALU.add,
                    op1=ALU.mult,
                )
            kept["t", u] = t

        def features_to_partitions(u):
            tT_ps = psum.tile([P, HALVES, PAIR * P], F32)
            for j in range(HALVES):
                for i in range(PAIR):
                    nc.tensor.transpose(
                        tT_ps[:, j, i * P : (i + 1) * P],
                        kept["t", u][:, i, j * P : (j + 1) * P],
                        ident[:],
                    )
            kept["tT", u] = tT_ps

        def gain_and_shift(u):
            yT = work.tile([P, HALVES, PAIR * P], F32)
            for j in range(HALVES):
                nc.scalar.activation(
                    out=yT[:, j, :],
                    in_=kept["tT", u][:, j, :],
                    func=ACT.Identity,
                    scale=norm_cols[:, j : j + 1],
                    bias=norm_cols[:, HALVES + j : HALVES + j + 1],
                )
            kept["yT", u] = yT

        def rows_to_partitions(u):
            y_ps = psum.tile([P, PAIR, FEAT], F32)
            for i in range(PAIR):
                for j in range(HALVES):
                    nc.tensor.transpose(
                        y_ps[:, i, j * P : (j + 1) * P],
                        kept["yT", u][:, j, i * P : (i + 1) * P],
                        ident[:],
                    )
            kept["y", u] = y_ps

        def add_residual_and_store(u):
            first = (u * PAIR % CHUNK) * FEAT
            result = results.tile([P, PAIR * FEAT], F32)
            nc.vector.tensor_tensor(
                out=result[:],
                in0=kept["y", u][:].rearrange("p i n -> p (i n)"),
                in1=x_chunks[u * PAIR // CHUNK][:, first : first + PAIR * FEAT],
                op=ALU.add,
            )
            nc.sync.dma_start(
                out=out_rows[:, u * PAIR : (u + 1) * PAIR, :],
                in_=result[:].rearrange("p (i n) -> p i n", i=PAIR),
            )

        stages = [
            transpose_h,
            regroup_h,
            quantise_h,
            project,
            add_bias,
            negate_mean,
            sum_squares,
            inverse_root,
            normalise,
            features_to_partitions,
            gain_and_shift,
            rows_to_partitions,
            add_residual_and_store,
        ]

        def one_round(s):
            for n, stage in reversed(list(enumerate(stages))):
                if 0 <= s - n < PAIRS:
                    stage(s - n)

        first_product = stages.index(project)
        for s in range(first_product):
            one_round(s)
        spread_constants()
        for s in range(first_product, PAIRS + len(stages) - 1):
            one_round(s)
